import numpy as np
import ml_dtypes

BF16 = ml_dtypes.bfloat16


def bf(x):
    return np.asarray(x, np.float32).astype(BF16)


def f32(x):
    return np.asarray(x, np.float32)


def f64(x):
    return np.asarray(x).astype(np.float64)


def striped(idx):
    return np.tile(idx.reshape(-1, 16).T, (8, 1))


C, S, N, D, RANK, NS = 512, 512, 256, 128, 64, 4


def setup_inputs():
    return {"base": f32(0.5 * np.random.standard_normal((C, S))), "kv": f32(np.random.standard_normal((C, N))), "logits": f32(0.5 * np.random.standard_normal((1, NS))), "offs": striped(np.random.permutation(S)[:N])}


def reference(base, kv, logits, offs):
    idx = offs[:16].T.reshape(-1)
    e = np.exp(f64(logits)[0])
    p = e / e.sum()
    r = (np.arange(C) % D < RANK).astype(np.float64)[:, None]
    out = f64(base).copy()
    out[:, idx] = (p[0] + p[1] * r) * f64(kv)
    return out

@@ -1,0 +1,59 @@
+import concourse.mybir as mybir
+
+P = 128
+C, S, N = 512, 512, 256
+BLOCKS = C // P
+RANK = 64
+NS = 4
+
+F32 = mybir.dt.float32
+U16 = mybir.dt.uint16
+MULT = mybir.AluOpType.mult
+ADD = mybir.AluOpType.add
+
+
+def tile_multistrategykvcache_kernel(tc, base, kv, logits, offs, out):
+    nc = tc.nc
+    with (
+        tc.tile_pool(name="held", bufs=1) as held,
+        tc.tile_pool(name="blocks", bufs=BLOCKS) as blocks,
+    ):
+        offsets = held.tile([P, N // 16], U16, name="offsets")
+        nc.sync.dma_start(offsets[:], offs)
+        scores = held.tile([P, NS], F32, name="scores")
+        nc.scalar.dma_start(scores[:], logits.to_broadcast([P, NS]))
+
+        windows = []
+        tokens = []
+        for b in range(BLOCKS):
+            rows = slice(b * P, (b + 1) * P)
+            window = blocks.tile([P, S], F32, name="window")
+            nc.sync.dma_start(window[:], base[rows, :])
+            windows.append(window)
+            token = blocks.tile([P, N], F32, name="token")
+            nc.scalar.dma_start(token[:], kv[rows, :])
+            tokens.append(token)
+
+        in_rank = held.tile([P, N], F32, name="in_rank")
+        nc.gpsimd.memset(in_rank[0:RANK, :], 1.0)
+        nc.gpsimd.memset(in_rank[RANK:P, :], 0.0)
+
+        neg_max = held.tile([P, 1], F32, name="neg_max")
+        nc.vector.reduce_max(neg_max[:], scores[:], axis=mybir.AxisListType.X, negate=True)
+        e = held.tile([P, NS], F32, name="e")
+        total = held.tile([P, 1], F32, name="total")
+        nc.scalar.activation(
+            e[:], scores[:], mybir.ActivationFunctionType.Exp, bias=neg_max[:], accum_out=total[:]
+        )
+        inv_total = held.tile([P, 1], F32, name="inv_total")
+        nc.vector.reciprocal(inv_total[:], total[:])
+        p = held.tile([P, NS], F32, name="p")
+        nc.vector.tensor_scalar(p[:], e[:], inv_total[:], None, op0=MULT)
+        weight = held.tile([P, N], F32, name="weight")
+        nc.vector.tensor_scalar(weight[:], in_rank[:], p[:, 1:2], p[:, 0:1], op0=MULT, op1=ADD)
+
+        for b in range(BLOCKS):
+            nc.vector.tensor_tensor(
+                windows[b][:].indirect(offsets[:]), tokens[b][:], weight[:], MULT
+            )
+            nc.sync.dma_start(out[b * P : (b + 1) * P, :], windows[b][:])

@@ -34,6 +34,11 @@ def tile_multistrategykvcache_kernel(tc, base, kv, logits, offs, out):
             nc.scalar.dma_start(token[:], kv[rows, :])
             tokens.append(token)
 
+        zero = held.tile([P, 1], F32, name="zero")
+        nc.gpsimd.memset(zero[:], 0.0)
+        one = held.tile([P, 1], F32, name="one")
+        nc.scalar.activation(one[:], zero[:], mybir.ActivationFunctionType.Exp)
+
         in_rank = held.tile([P, N], F32, name="in_rank")
         nc.gpsimd.memset(in_rank[0:RANK, :], 1.0)
         nc.gpsimd.memset(in_rank[RANK:P, :], 0.0)

@@ -10,34 +10,31 @@ F32 = mybir.dt.float32
 U16 = mybir.dt.uint16
 MULT = mybir.AluOpType.mult
 ADD = mybir.AluOpType.add
+EXP = mybir.ActivationFunctionType.Exp
 
 
 def tile_multistrategykvcache_kernel(tc, base, kv, logits, offs, out):
     nc = tc.nc
-    with (
-        tc.tile_pool(name="held", bufs=1) as held,
-        tc.tile_pool(name="blocks", bufs=BLOCKS) as blocks,
-    ):
-        offsets = held.tile([P, N // 16], U16, name="offsets")
-        nc.sync.dma_start(offsets[:], offs)
+    with tc.tile_pool(name="held", bufs=1) as held:
         scores = held.tile([P, NS], F32, name="scores")
         nc.scalar.dma_start(scores[:], logits.to_broadcast([P, NS]))
-
-        windows = []
-        tokens = []
-        for b in range(BLOCKS):
-            rows = slice(b * P, (b + 1) * P)
-            window = blocks.tile([P, S], F32, name="window")
-            nc.sync.dma_start(window[:], base[rows, :])
-            windows.append(window)
-            token = blocks.tile([P, N], F32, name="token")
-            nc.scalar.dma_start(token[:], kv[rows, :])
-            tokens.append(token)
-
         zero = held.tile([P, 1], F32, name="zero")
         nc.gpsimd.memset(zero[:], 0.0)
         one = held.tile([P, 1], F32, name="one")
-        nc.scalar.activation(one[:], zero[:], mybir.ActivationFunctionType.Exp)
+        nc.scalar.activation(one[:], zero[:], EXP)
+
+        offsets = held.tile([P, N // 16], U16, name="offsets")
+        nc.sync.dma_start(offsets[:], offs)
+        windows = []
+        tokens = []
+        for b in range(BLOCKS):
+            if b % 2 == 0:
+                pair = held.tile([P, 2, N], F32, name=f"pair{b // 2}")
+                nc.sync.dma_start(pair[:], kv[b * P : (b + 2) * P, :].rearrange("(t p) n -> p t n", p=P))
+            tokens.append(pair[:, b % 2, :])
+            window = held.tile([P, S], F32, name=f"window{b}")
+            nc.sync.dma_start(window[:], base[b * P : (b + 1) * P, :])
+            windows.append(window)
 
         in_rank = held.tile([P, N], F32, name="in_rank")
         nc.gpsimd.memset(in_rank[0:RANK, :], 1.0)
@@ -47,9 +44,7 @@ def tile_multistrategykvcache_kernel(tc, base, kv, logits, offs, out):
         nc.vector.reduce_max(neg_max[:], scores[:], axis=mybir.AxisListType.X, negate=True)
         e = held.tile([P, NS], F32, name="e")
         total = held.tile([P, 1], F32, name="total")
-        nc.scalar.activation(
-            e[:], scores[:], mybir.ActivationFunctionType.Exp, bias=neg_max[:], accum_out=total[:]
-        )
+        nc.scalar.activation(e[:], scores[:], EXP, bias=neg_max[:], accum_out=total[:])
         inv_total = held.tile([P, 1], F32, name="inv_total")
         nc.vector.reciprocal(inv_total[:], total[:])
         p = held.tile([P, NS], F32, name="p")
@@ -58,7 +53,5 @@ def tile_multistrategykvcache_kernel(tc, base, kv, logits, offs, out):
         nc.vector.tensor_scalar(weight[:], in_rank[:], p[:, 1:2], p[:, 0:1], op0=MULT, op1=ADD)
 
         for b in range(BLOCKS):
-            nc.vector.tensor_tensor(
-                windows[b][:].indirect(offsets[:]), tokens[b][:], weight[:], MULT
-            )
+            nc.vector.tensor_tensor(windows[b][:].indirect(offsets[:]), tokens[b], weight[:], MULT)
             nc.sync.dma_start(out[b * P : (b + 1) * P, :], windows[b][:])

@@ -36,21 +36,23 @@ def tile_multistrategykvcache_kernel(tc, base, kv, logits, offs, out):
             nc.sync.dma_start(window[:], base[b * P : (b + 1) * P, :])
             windows.append(window)
 
-        in_rank = held.tile([P, N], F32, name="in_rank")
+        in_rank = held.tile([P, 1], F32, name="in_rank")
         nc.gpsimd.memset(in_rank[0:RANK, :], 1.0)
         nc.gpsimd.memset(in_rank[RANK:P, :], 0.0)
+        ones = held.tile([P, N], F32, name="ones")
+        nc.gpsimd.memset(ones[:], 1.0)
 
         neg_max = held.tile([P, 1], F32, name="neg_max")
         nc.vector.reduce_max(neg_max[:], scores[:], axis=mybir.AxisListType.X, negate=True)
         e = held.tile([P, NS], F32, name="e")
         total = held.tile([P, 1], F32, name="total")
         nc.scalar.activation(e[:], scores[:], EXP, bias=neg_max[:], accum_out=total[:])
+        blend = held.tile([P, 1], F32, name="blend")
+        nc.vector.tensor_scalar(blend[:], in_rank[:], e[:, 1:2], e[:, 0:1], op0=MULT, op1=ADD)
         inv_total = held.tile([P, 1], F32, name="inv_total")
         nc.vector.reciprocal(inv_total[:], total[:])
-        p = held.tile([P, NS], F32, name="p")
-        nc.vector.tensor_scalar(p[:], e[:], inv_total[:], None, op0=MULT)
         weight = held.tile([P, N], F32, name="weight")
-        nc.vector.tensor_scalar(weight[:], in_rank[:], p[:, 1:2], p[:, 0:1], op0=MULT, op1=ADD)
+        nc.vector.tensor_scalar(weight[:], ones[:], blend[:], inv_total[:], op0=MULT, op1=MULT)
 
         for b in range(BLOCKS):
             nc.vector.tensor_tensor(windows[b][:].indirect(offsets[:]), tokens[b], weight[:], MULT)

@@ -25,16 +25,15 @@ def tile_multistrategykvcache_kernel(tc, base, kv, logits, offs, out):
 
         offsets = held.tile([P, N // 16], U16, name="offsets")
         nc.sync.dma_start(offsets[:], offs)
-        windows = []
-        tokens = []
-        for b in range(BLOCKS):
-            if b % 2 == 0:
-                pair = held.tile([P, 2, N], F32, name=f"pair{b // 2}")
-                nc.sync.dma_start(pair[:], kv[b * P : (b + 2) * P, :].rearrange("(t p) n -> p t n", p=P))
-            tokens.append(pair[:, b % 2, :])
-            window = held.tile([P, S], F32, name=f"window{b}")
-            nc.sync.dma_start(window[:], base[b * P : (b + 1) * P, :])
-            windows.append(window)
+        first = held.tile([P, N], F32, name="first")
+        nc.sync.dma_start(first[:], kv[0:P, :])
+        windows = [held.tile([P, S], F32, name=f"window{b}") for b in range(BLOCKS)]
+        nc.sync.dma_start(windows[0][:], base[0:P, :])
+        rest = held.tile([P, BLOCKS - 1, N], F32, name="rest")
+        nc.sync.dma_start(rest[:], kv[P:C, :].rearrange("(t p) n -> p t n", p=P))
+        for b in range(1, BLOCKS):
+            nc.sync.dma_start(windows[b][:], base[b * P : (b + 1) * P, :])
+        tokens = [first[:]] + [rest[:, b - 1, :] for b in range(1, BLOCKS)]
 
         in_rank = held.tile([P, 1], F32, name="in_rank")
         nc.gpsimd.memset(in_rank[0:RANK, :], 1.0)

@@ -17,7 +17,7 @@ def tile_multistrategykvcache_kernel(tc, base, kv, logits, offs, out):
     nc = tc.nc
     with tc.tile_pool(name="held", bufs=1) as held:
         scores = held.tile([P, NS], F32, name="scores")
-        nc.scalar.dma_start(scores[:], logits.to_broadcast([P, NS]))
+        nc.sync.dma_start(scores[:], logits.to_broadcast([P, NS]))
         zero = held.tile([P, 1], F32, name="zero")
         nc.gpsimd.memset(zero[:], 0.0)
         one = held.tile([P, 1], F32, name="one")
@@ -25,15 +25,16 @@ def tile_multistrategykvcache_kernel(tc, base, kv, logits, offs, out):
 
         offsets = held.tile([P, N // 16], U16, name="offsets")
         nc.sync.dma_start(offsets[:], offs)
-        first = held.tile([P, N], F32, name="first")
-        nc.sync.dma_start(first[:], kv[0:P, :])
-        windows = [held.tile([P, S], F32, name=f"window{b}") for b in range(BLOCKS)]
-        nc.sync.dma_start(windows[0][:], base[0:P, :])
-        rest = held.tile([P, BLOCKS - 1, N], F32, name="rest")
-        nc.sync.dma_start(rest[:], kv[P:C, :].rearrange("(t p) n -> p t n", p=P))
-        for b in range(1, BLOCKS):
-            nc.sync.dma_start(windows[b][:], base[b * P : (b + 1) * P, :])
-        tokens = [first[:]] + [rest[:, b - 1, :] for b in range(1, BLOCKS)]
+        windows = []
+        tokens = []
+        for b in range(BLOCKS):
+            if b % 2 == 0:
+                pair = held.tile([P, 2, N], F32, name=f"pair{b // 2}")
+                nc.sync.dma_start(pair[:], kv[b * P : (b + 2) * P, :].rearrange("(t p) n -> p t n", p=P))
+            tokens.append(pair[:, b % 2, :])
+            window = held.tile([P, S], F32, name=f"window{b}")
+            nc.sync.dma_start(window[:], base[b * P : (b + 1) * P, :])
+            windows.append(window)
 
         in_rank = held.tile([P, 1], F32, name="in_rank")
         nc.gpsimd.memset(in_rank[0:RANK, :], 1.0)

@@ -28,10 +28,9 @@ def tile_multistrategykvcache_kernel(tc, base, kv, logits, offs, out):
         windows = []
         tokens = []
         for b in range(BLOCKS):
-            if b % 2 == 0:
-                pair = held.tile([P, 2, N], F32, name=f"pair{b // 2}")
-                nc.sync.dma_start(pair[:], kv[b * P : (b + 2) * P, :].rearrange("(t p) n -> p t n", p=P))
-            tokens.append(pair[:, b % 2, :])
+            token = held.tile([P, N], F32, name=f"token{b}")
+            nc.sync.dma_start(token[:], kv[b * P : (b + 1) * P, :])
+            tokens.append(token)
             window = held.tile([P, S], F32, name=f"window{b}")
             nc.sync.dma_start(window[:], base[b * P : (b + 1) * P, :])
             windows.append(window)
@@ -55,5 +54,5 @@ def tile_multistrategykvcache_kernel(tc, base, kv, logits, offs, out):
         nc.vector.tensor_scalar(weight[:], ones[:], blend[:], inv_total[:], op0=MULT, op1=MULT)
 
         for b in range(BLOCKS):
-            nc.vector.tensor_tensor(windows[b][:].indirect(offsets[:]), tokens[b], weight[:], MULT)
+            nc.vector.tensor_tensor(windows[b][:].indirect(offsets[:]), tokens[b][:], weight[:], MULT)
             nc.sync.dma_start(out[b * P : (b + 1) * P, :], windows[b][:])

@@ -19,7 +19,7 @@ def tile_multistrategykvcache_kernel(tc, base, kv, logits, offs, out):
         scores = held.tile([P, NS], F32, name="scores")
         nc.sync.dma_start(scores[:], logits.to_broadcast([P, NS]))
         zero = held.tile([P, 1], F32, name="zero")
-        nc.gpsimd.memset(zero[:], 0.0)
+        nc.vector.memset(zero[:], 0.0)
         one = held.tile([P, 1], F32, name="one")
         nc.scalar.activation(one[:], zero[:], EXP)
 
@@ -36,10 +36,10 @@ def tile_multistrategykvcache_kernel(tc, base, kv, logits, offs, out):
             windows.append(window)
 
         in_rank = held.tile([P, 1], F32, name="in_rank")
-        nc.gpsimd.memset(in_rank[0:RANK, :], 1.0)
-        nc.gpsimd.memset(in_rank[RANK:P, :], 0.0)
+        nc.vector.memset(in_rank[0:RANK, :], 1.0)
+        nc.vector.memset(in_rank[RANK:P, :], 0.0)
         ones = held.tile([P, N], F32, name="ones")
-        nc.gpsimd.memset(ones[:], 1.0)
+        nc.vector.memset(ones[:], 1.0)
 
         neg_max = held.tile([P, 1], F32, name="neg_max")
         nc.vector.reduce_max(neg_max[:], scores[:], axis=mybir.AxisListType.X, negate=True)

@@ -29,10 +29,15 @@ def tile_multistrategykvcache_kernel(tc, base, kv, logits, offs, out):
         tokens = []
         for b in range(BLOCKS):
             token = held.tile([P, N], F32, name=f"token{b}")
-            nc.sync.dma_start(token[:], kv[b * P : (b + 1) * P, :])
+            halves = 2 if b == BLOCKS - 1 else 1
+            for h in range(halves):
+                cols = slice(h * N // halves, (h + 1) * N // halves)
+                nc.sync.dma_start(token[:, cols], kv[b * P : (b + 1) * P, cols])
             tokens.append(token)
             window = held.tile([P, S], F32, name=f"window{b}")
-            nc.sync.dma_start(window[:], base[b * P : (b + 1) * P, :])
+            for h in range(halves):
+                cols = slice(h * S // halves, (h + 1) * S // halves)
+                nc.sync.dma_start(window[:, cols], base[b * P : (b + 1) * P, cols])
             windows.append(window)
 
         in_rank = held.tile([P, 1], F32, name="in_rank")

@@ -43,8 +43,6 @@ def tile_multistrategykvcache_kernel(tc, base, kv, logits, offs, out):
         in_rank = held.tile([P, 1], F32, name="in_rank")
         nc.vector.memset(in_rank[0:RANK, :], 1.0)
         nc.vector.memset(in_rank[RANK:P, :], 0.0)
-        ones = held.tile([P, N], F32, name="ones")
-        nc.vector.memset(ones[:], 1.0)
 
         neg_max = held.tile([P, 1], F32, name="neg_max")
         nc.vector.reduce_max(neg_max[:], scores[:], axis=mybir.AxisListType.X, negate=True)
@@ -56,7 +54,7 @@ def tile_multistrategykvcache_kernel(tc, base, kv, logits, offs, out):
         inv_total = held.tile([P, 1], F32, name="inv_total")
         nc.vector.reciprocal(inv_total[:], total[:])
         weight = held.tile([P, N], F32, name="weight")
-        nc.vector.tensor_scalar(weight[:], ones[:], blend[:], inv_total[:], op0=MULT, op1=MULT)
+        nc.vector.tensor_scalar(weight[:], blend[:].to_broadcast([P, N]), inv_total[:], None, op0=MULT)
 
         for b in range(BLOCKS):
             nc.vector.tensor_tensor(windows[b][:].indirect(offsets[:]), tokens[b][:], weight[:], MULT)

@@ -9,6 +9,7 @@ NS = 4
 F32 = mybir.dt.float32
 U16 = mybir.dt.uint16
 MULT = mybir.AluOpType.mult
+MAX = mybir.AluOpType.max
 ADD = mybir.AluOpType.add
 EXP = mybir.ActivationFunctionType.Exp
 
@@ -44,11 +45,11 @@ def tile_multistrategykvcache_kernel(tc, base, kv, logits, offs, out):
         nc.vector.memset(in_rank[0:RANK, :], 1.0)
         nc.vector.memset(in_rank[RANK:P, :], 0.0)
 
-        neg_max = held.tile([P, 1], F32, name="neg_max")
-        nc.vector.reduce_max(neg_max[:], scores[:], axis=mybir.AxisListType.X, negate=True)
+        neg_shift = held.tile([P, 1], F32, name="neg_shift")
+        nc.vector.tensor_scalar(neg_shift[:], scores[:, 0:1], scores[:, 1:2], -1.0, op0=MAX, op1=MULT)
         e = held.tile([P, NS], F32, name="e")
         total = held.tile([P, 1], F32, name="total")
-        nc.scalar.activation(e[:], scores[:], EXP, bias=neg_max[:], accum_out=total[:])
+        nc.scalar.activation(e[:], scores[:], EXP, bias=neg_shift[:], accum_out=total[:])
         blend = held.tile([P, 1], F32, name="blend")
         nc.vector.tensor_scalar(blend[:], in_rank[:], e[:, 1:2], e[:, 0:1], op0=MULT, op1=ADD)
         inv_total = held.tile([P, 1], F32, name="inv_total")

@@ -50,10 +50,10 @@ def tile_multistrategykvcache_kernel(tc, base, kv, logits, offs, out):
         e = held.tile([P, NS], F32, name="e")
         total = held.tile([P, 1], F32, name="total")
         nc.scalar.activation(e[:], scores[:], EXP, bias=neg_shift[:], accum_out=total[:])
-        blend = held.tile([P, 1], F32, name="blend")
-        nc.vector.tensor_scalar(blend[:], in_rank[:], e[:, 1:2], e[:, 0:1], op0=MULT, op1=ADD)
         inv_total = held.tile([P, 1], F32, name="inv_total")
         nc.vector.reciprocal(inv_total[:], total[:])
+        blend = held.tile([P, 1], F32, name="blend")
+        nc.vector.tensor_scalar(blend[:], in_rank[:], e[:, 1:2], e[:, 0:1], op0=MULT, op1=ADD)
         weight = held.tile([P, N], F32, name="weight")
         nc.vector.tensor_scalar(weight[:], blend[:].to_broadcast([P, N]), inv_total[:], None, op0=MULT)
 

import concourse.mybir as mybir

P = 128
C, S, N = 512, 512, 256
BLOCKS = C // P
RANK = 64
NS = 4

F32 = mybir.dt.float32
U16 = mybir.dt.uint16
MULT = mybir.AluOpType.mult
MAX = mybir.AluOpType.max
ADD = mybir.AluOpType.add
EXP = mybir.ActivationFunctionType.Exp


def tile_multistrategykvcache_kernel(tc, base, kv, logits, offs, out):
    nc = tc.nc
    with tc.tile_pool(name="held", bufs=1) as held:
        scores = held.tile([P, NS], F32, name="scores")
        nc.sync.dma_start(scores[:], logits.to_broadcast([P, NS]))
        zero = held.tile([P, 1], F32, name="zero")
        nc.vector.memset(zero[:], 0.0)
        one = held.tile([P, 1], F32, name="one")
        nc.scalar.activation(one[:], zero[:], EXP)

        offsets = held.tile([P, N // 16], U16, name="offsets")
        nc.sync.dma_start(offsets[:], offs)
        windows = []
        tokens = []
        for b in range(BLOCKS):
            token = held.tile([P, N], F32, name=f"token{b}")
            halves = 2 if b == BLOCKS - 1 else 1
            for h in range(halves):
                cols = slice(h * N // halves, (h + 1) * N // halves)
                nc.sync.dma_start(token[:, cols], kv[b * P : (b + 1) * P, cols])
            tokens.append(token)
            window = held.tile([P, S], F32, name=f"window{b}")
            for h in range(halves):
                cols = slice(h * S // halves, (h + 1) * S // halves)
                nc.sync.dma_start(window[:, cols], base[b * P : (b + 1) * P, cols])
            windows.append(window)

        in_rank = held.tile([P, 1], F32, name="in_rank")
        nc.vector.memset(in_rank[0:RANK, :], 1.0)
        nc.vector.memset(in_rank[RANK:P, :], 0.0)

        neg_shift = held.tile([P, 1], F32, name="neg_shift")
        nc.vector.tensor_scalar(neg_shift[:], scores[:, 0:1], scores[:, 1:2], -1.0, op0=MAX, op1=MULT)
        e = held.tile([P, NS], F32, name="e")
        total = held.tile([P, 1], F32, name="total")
        nc.scalar.activation(e[:], scores[:], EXP, bias=neg_shift[:], accum_out=total[:])
        inv_total = held.tile([P, 1], F32, name="inv_total")
        nc.vector.reciprocal(inv_total[:], total[:])
        blend = held.tile([P, 1], F32, name="blend")
        nc.vector.tensor_scalar(blend[:], in_rank[:], e[:, 1:2], e[:, 0:1], op0=MULT, op1=ADD)
        weight = held.tile([P, N], F32, name="weight")
        nc.vector.tensor_scalar(weight[:], blend[:].to_broadcast([P, N]), inv_total[:], None, op0=MULT)

        for b in range(BLOCKS):
            nc.vector.tensor_tensor(windows[b][:].indirect(offsets[:]), tokens[b][:], weight[:], MULT)
            nc.sync.dma_start(out[b * P : (b + 1) * P, :], windows[b][:])
